import numpy as np
import ml_dtypes


def mxq(x, axis, fmt="e4m3"):
    dtype, down = {"e4m3": (ml_dtypes.float8_e4m3fn, 7), "e5m2": (ml_dtypes.float8_e5m2, 14)}[fmt]
    v = np.moveaxis(np.asarray(x, np.float32).astype(ml_dtypes.bfloat16).astype(np.float64), axis, -1)
    blocks = v.reshape(v.shape[:-1] + (-1, 32))
    amax = np.abs(blocks).max(-1, keepdims=True)
    byte = np.maximum(np.where(amax > 0, np.frexp(amax)[1] - 1 + 127, 0) - down, 1)
    scale = np.exp2(byte - 127.0)
    codes = (blocks / scale).astype(np.float32).astype(dtype).astype(np.float64)
    return np.moveaxis((codes * scale).reshape(v.shape), -1, axis)


WIDE = False


def mx_kscale(k):
    if not WIDE:
        return np.ones(k)
    levels = np.array([18, -18])
    if k % 512:
        return np.exp2(np.random.permutation(np.resize(levels, k // 32))).repeat(32)
    a = np.empty((k // 512, 16))
    for p in range(k // 512):
        a[p, :8] = np.random.permutation(np.resize(levels, 8))
        for g in range(8):
            far = levels[np.abs(levels - a[p, g]) >= 10]
            a[p, g + 8] = far[np.random.randint(len(far))]
    return np.exp2(a.ravel()).repeat(32)


BF16 = ml_dtypes.bfloat16


def bf(x):
    return np.asarray(x, np.float32).astype(BF16)


def f64(x):
    return np.asarray(x).astype(np.float64)


B, H, L, DM, DK = 2, 2, 512, 512, 512
T = B * H * L


def rotate_every_two(x):
    x1 = x[..., ::2]
    x2 = x[..., 1::2]
    return np.stack((-x2, x1), axis=-1).reshape(x.shape)


def xpos_sincos(length, dim):
    angle = 1.0 / (10000.0 ** np.linspace(0.0, 1.0, dim // 2))
    angle = np.repeat(angle, 2)
    idx = f64(np.arange(length))
    angles = idx[:, None] * angle[None, :]
    return np.sin(angles), np.cos(angles)


def setup_inputs():
    s = mx_kscale(T).reshape(B, H, L, 1)
    u = mx_kscale(2 * DK)
    uq, uk = u[:DK], u[DK:]
    X0 = bf(np.random.standard_normal((B, H, L, DM)))
    WQ0 = bf(np.random.standard_normal((DM, DK)) * 3.0 / np.sqrt(DM))
    WK0 = bf(np.random.standard_normal((DM, DK)) * 3.0 / np.sqrt(DM))
    g0 = bf(np.random.standard_normal((B, H, L, DK)) * np.exp2(np.random.randint(-6, 1, (B, H, L, 1))) / s * uq)
    g1 = bf(np.random.standard_normal((B, H, L, DK)) * np.exp2(np.random.randint(-6, 1, (B, H, L, 1))) / s * uk)
    return {"X": bf(f64(X0) * s),
            "W_Q": bf(f64(WQ0) / uq),
            "W_K": bf(f64(WK0) / uk),
            "grad_0": g0,
            "grad_1": g1}


def reference(X, W_Q, W_K, grad_0, grad_1):
    sin, cos = xpos_sincos(L, DK)
    g0 = f64(grad_0)
    g1 = f64(grad_1)
    dq = g0 * cos - rotate_every_two(g0) * sin
    dk = g1 * cos + rotate_every_two(g1) * sin
    dz = np.concatenate([dq.reshape(T, DK), dk.reshape(T, DK)], axis=1)
    w = np.concatenate([f64(W_Q), f64(W_K)], axis=1)
    dx = mxq(dz, 1, "e5m2") @ mxq(w, 1, "e4m3").T
    xt = mxq(f64(X).reshape(T, DM), 0, "e4m3")
    dw = xt.T @ mxq(dz, 0, "e5m2")
    return dx.reshape(B, H, L, DM), dw[:, :DK], dw[:, DK:]

@@ -1,0 +1,312 @@
+import math
+from contextlib import ExitStack
+
+import concourse.mybir as mybir
+from concourse.masks import make_identity
+
+F32 = mybir.dt.float32
+BF16 = mybir.dt.bfloat16
+I32 = mybir.dt.int32
+U32 = mybir.dt.uint32
+U8 = mybir.dt.uint8
+E4M3 = mybir.dt.float8_e4m3fn_x4
+E5M2 = mybir.dt.float8_e5m2_x4
+ALU = mybir.AluOpType
+SIN = mybir.ActivationFunctionType.Sin
+
+P = 128
+SEQS = 4
+L = 512
+D = 512
+STEPS = 16
+FLOPS = 2 * 2 * (SEQS * L) * (2 * D) * D
+
+
+def tile_retention_pa_v_kernel(tc, X, W_Q, W_K, grad_0, grad_1, out_0, out_1, out_2):
+    nc = tc.nc
+    quad = "b h (p j) f -> (b h) p j f"
+    x_hbm = X.rearrange(quad, j=4)
+    g_hbm = [grad_0.rearrange(quad, j=4), grad_1.rearrange(quad, j=4)]
+    dx_hbm = out_0.rearrange(quad, j=4)
+    w_hbm = [W_Q.rearrange("(a r) f -> r a f", r=P), W_K.rearrange("(a r) f -> r a f", r=P)]
+    dw_hbm = [out_1, out_2]
+
+    with ExitStack() as ctx:
+        keep = ctx.enter_context(tc.tile_pool(name="keep", bufs=1))
+        ring = ctx.enter_context(tc.tile_pool(name="ring", bufs=2))
+        outs = ctx.enter_context(tc.tile_pool(name="outs", bufs=4))
+        psum = ctx.enter_context(tc.psum_pool(name="psum", bufs=1))
+        ctx.enter_context(tc.manual_schedule())
+
+        def bank(tag, shape):
+            return psum.tile(shape, F32, name=tag, tag=tag)
+
+        def mx_pair(name, width):
+            codes = keep.tile([P, width], U32, name=name + "_codes", align_bytes=64)
+            scales = keep.tile([P, width], U8, name=name + "_scales", align_bytes=64)
+            return codes, scales
+
+        def quantize(pair, fmt, src):
+            nc.vector.quantize_mx(out=pair[0][:].bitcast(fmt), scales=pair[1][:], in_=src[:])
+
+        g_raw, x_raw, w_raw = {}, {}, {}
+
+        def load_g(s):
+            g_raw[s] = keep.tile([P, 2, D], BF16, name="g_raw%d" % s, align_bytes=64)
+            nc.sync.dma_start(out=g_raw[s][:], in_=g_hbm[s // 8][(s // 2) % SEQS][:, 2 * (s % 2) : 2 * (s % 2) + 2, :])
+
+        def load_x(q):
+            x_raw[q] = keep.tile([P, 4, D], BF16, name="x_raw%d" % q, align_bytes=64)
+            nc.sync.dma_start(out=x_raw[q][:], in_=x_hbm[q])
+
+        def load_w(w):
+            w_raw[w] = keep.tile([P, 4, D], BF16, name="w_raw%d" % w, align_bytes=64)
+            nc.sync.dma_start(out=w_raw[w][:], in_=w_hbm[w])
+
+        for q in range(SEQS):
+            load_g(2 * q)
+            load_g(2 * q + 1)
+            load_x(q)
+            if q == 1:
+                load_w(0)
+                load_w(1)
+        for s in range(8, STEPS):
+            load_g(s)
+
+        ident = keep.tile([P, P], F32, name="ident")
+        make_identity(nc, ident[:])
+        pos = keep.tile([P, L], F32, name="pos")
+        nc.gpsimd.iota(pos[:], pattern=[[1, 4], [4, P]], base=0, channel_multiplier=0, allow_small_or_imprecise_dtypes=True)
+
+        ratio = 10000.0 ** (-1.0 / 255.0)
+        one = keep.tile([P, 1], F32, name="one")
+        nc.vector.memset(one[:], 1.0)
+        turns_row = keep.tile([P, 256], F32, name="turns_row")
+        for b in range(8):
+            nc.vector.tensor_scalar(out=turns_row[:, b : b + 1], in0=one[:], scalar1=ratio**b / (2 * math.pi), scalar2=None, op0=ALU.mult)
+        for have, copies in ((8, 8), (64, 4)):
+            for a in range(1, copies):
+                nc.vector.tensor_scalar(
+                    out=turns_row[:, a * have : (a + 1) * have], in0=turns_row[:, :have], scalar1=ratio ** (a * have), scalar2=None, op0=ALU.mult
+                )
+        turns_ps = bank("acc0", [P, 2, P])
+        for h in range(2):
+            nc.tensor.transpose(turns_ps[:, h, :], turns_row[:, h::2], ident[:])
+        turns = keep.tile([P, 2], F32, name="turns")
+        nc.vector.tensor_copy(out=turns[:], in_=turns_ps[:, :, 0])
+
+        whole = [keep.tile([P, L], I32, name="whole%d" % h) for h in range(2)]
+        for h in range(2):
+            nc.vector.tensor_scalar(out=whole[h][:], in0=pos[:], scalar1=turns[:, h : h + 1], scalar2=None, op0=ALU.mult)
+        table = []
+        for a in range(2):
+            cols = slice(256 * a, 256 * (a + 1))
+            frac = keep.tile([P, 2, 256], F32, name="frac%d" % a)
+            size = keep.tile([P, 2, 256], F32, name="size%d" % a)
+            for h in range(2):
+                nc.vector.scalar_tensor_tensor(
+                    out=frac[:, h, :], in0=pos[:, cols], scalar=turns[:, h : h + 1], in1=whole[h][:, cols], op0=ALU.mult, op1=ALU.subtract
+                )
+            nc.vector.scalar_tensor_tensor(out=size[:], in0=frac[:], scalar=-1.0, in1=frac[:], op0=ALU.mult, op1=ALU.max)
+            tab = keep.tile([P, 3, 256, 2], F32, name="table%d" % a)
+            frac_nh = frac[:].rearrange("p h n -> p n h")
+            size_nh = size[:].rearrange("p h n -> p n h")
+            nc.scalar.activation(out=tab[:, 0], in_=frac_nh, func=SIN, scale=2 * math.pi)
+            nc.scalar.activation(out=tab[:, 1], in_=size_nh, func=SIN, scale=-2 * math.pi, bias=math.pi / 2)
+            nc.scalar.activation(out=tab[:, 2], in_=frac_nh, func=SIN, scale=-2 * math.pi)
+            table.append(tab)
+
+        g_ps, prod, dz_f, back_ps, dz_t, x_t, w_ps, w_t = {}, {}, {}, {}, {}, {}, {}, {}
+        f_mx = [mx_pair("f%d" % s, 256) for s in range(STEPS)]
+        t_mx = [mx_pair("t%d" % t, D) for t in range(2 * SEQS)]
+        x_mx = [mx_pair("x%d" % q, D) for q in range(SEQS)]
+        w_mx = [mx_pair("w%d" % w, D) for w in range(2)]
+
+        def turn_g(s):
+            g_ps[s] = bank("fwd%d" % (s % 2), [P, 2, 2, P])
+            words = g_raw[s][:].rearrange("p j f -> p (j f)").bitcast(F32)
+            for j in range(2):
+                for h in range(2):
+                    nc.tensor.transpose(g_ps[s][:, h, j, :], words[:, 256 * j + h : 256 * (j + 1) : 2], ident[:])
+
+        def products(s):
+            tab = table[s % 2]
+            pairs = g_ps[s][:].rearrange("p h j r -> p (h j r)").bitcast(BF16).rearrange("p (h n e) -> p n h e", h=2, e=2)
+            if s < 8:
+                rows = {0: tab[:, 1:3], 1: tab[:, 0:2]}
+            else:
+                rows = {0: tab[:, 1::-1], 1: tab[:, 2:0:-1]}
+            prod[s] = {}
+            for e in (1, 0):
+                prod[s][e] = ring.tile([P, 256, 2, 2], F32, name="prod%d" % e, tag="prod%d" % e)
+                nc.vector.tensor_tensor(
+                    out=prod[s][e][:],
+                    in0=pairs[:, :, :, e : e + 1].to_broadcast([P, 256, 2, 2]),
+                    in1=rows[e].rearrange("p o n h -> p n h o"),
+                    op=ALU.mult,
+                )
+
+        def add(s, engine):
+            dz_f[s] = ring.tile([P, 1024], BF16, name="dz_f", tag="dz_f", align_bytes=64)
+            flat = "p n h o -> p (n h o)"
+            engine.tensor_tensor(out=dz_f[s][:], in0=prod[s][0][:].rearrange(flat), in1=prod[s][1][:].rearrange(flat), op=ALU.add)
+
+        def turn_back(s):
+            t = s // 2
+            if s % 2 == 0:
+                back_ps[t] = [bank("back%d" % h, [P, 4, P]) for h in range(2)]
+            words = dz_f[s][:].bitcast(F32)
+            for h in range(2):
+                for j in range(2):
+                    nc.tensor.transpose(back_ps[t][h][:, 2 * (s % 2) + j, :], words[:, 256 * j + h : 256 * (j + 1) : 2], ident[:])
+
+        def copy_on(engine, out, in_):
+            if engine == "scalar":
+                nc.scalar.copy(out=out, in_=in_)
+            else:
+                nc.vector.tensor_copy(out=out, in_=in_)
+
+        def group_tokens(t, h, engine="scalar"):
+            if h == 0:
+                dz_t[t] = ring.tile([P, 4 * D], BF16, name="dz_t", tag="dz_t", align_bytes=64)
+            src = back_ps[t][h][:].rearrange("p j r -> p (j r)").bitcast(BF16).rearrange("p (j r e) -> p r e j", j=4, e=2)
+            dst = dz_t[t][:].rearrange("p (r h e j) -> p h r e j", h=2, e=2, j=4)[:, h]
+            copy_on(engine, dst, src)
+
+        def group_x(q):
+            x_t[q] = ring.tile([P, 4 * D], BF16, name="x_t", tag="x_t", align_bytes=64)
+            nc.scalar.copy(
+                out=x_t[q][:].rearrange("p (c i j) -> p c j i", i=4, j=4),
+                in_=x_raw[q][:].rearrange("p j (c i) -> p c j i", i=4),
+            )
+
+        def turn_w(w):
+            words = w_raw[w][:].rearrange("r a f -> r (a f)").bitcast(F32)
+            w_ps[w] = [bank("acc%d" % (2 * w + b), [P, 2, 2, P]) for b in range(2)]
+            for a in range(4):
+                for h in range(2):
+                    nc.tensor.transpose(w_ps[w][a // 2][:, a % 2, h, :], words[:, 256 * a + h : 256 * (a + 1) : 2], ident[:])
+
+        def group_w(w):
+            w_t[w] = ring.tile([P, 4 * D], BF16, name="w_t", tag="w_t", align_bytes=64)
+            dst = w_t[w][:].bitcast(F32).rearrange("p (a r h) -> p a r h", a=4, h=2)
+            for b in range(2):
+                nc.scalar.copy(out=dst[:, 2 * b : 2 * b + 2], in_=w_ps[w][b][:].rearrange("p a h r -> p a r h"))
+
+        def mx_pass(acc, still, still_fmt, cols, moving, moving_fmt, start, stop):
+            nc.tensor.matmul_mx(
+                out=acc[:],
+                lhsT=still[0][:, cols].bitcast(still_fmt),
+                lhsT_scale=still[1][:, cols],
+                rhs=moving[0][:].bitcast(moving_fmt),
+                rhs_scale=moving[1][:],
+                start=start,
+                stop=stop,
+            )
+
+        dx_sb, dw_ps = {}, {}
+
+        def dx_tile(s, j, tag, engine="scalar"):
+            acc = bank(tag, [P, D])
+            for w in range(2):
+                mx_pass(acc, f_mx[s - 8 + 8 * w], E5M2, slice(P * j, P * (j + 1)), w_mx[w], E4M3, w == 0, w == 1)
+            if j == 0:
+                dx_sb[s] = outs.tile([P, 2, D], F32, name="dx_sb", tag="dx_sb")
+            copy_on(engine, dx_sb[s][:, j, :], acc[:])
+            if j == 1:
+                nc.sync.dma_start(out=dx_hbm[(s // 2) % SEQS][:, 2 * (s % 2) : 2 * (s % 2) + 2, :], in_=dx_sb[s][:])
+
+        def dw_pass(w, m, q, tag):
+            if q == 0:
+                dw_ps[w, m] = bank(tag, [P, D])
+            mx_pass(dw_ps[w, m], x_mx[q], E4M3, slice(P * m, P * (m + 1)), t_mx[SEQS * w + q], E5M2, q == 0, q == SEQS - 1)
+
+        def dw_out(w, m, engine="scalar"):
+            dw_sb = outs.tile([P, D], F32, name="dw_sb", tag="dw_sb")
+            copy_on(engine, dw_sb[:], dw_ps[w, m][:])
+            nc.sync.dma_start(out=dw_hbm[w][P * m : P * (m + 1), :], in_=dw_sb[:])
+
+        def quant_f(s):
+            quantize(f_mx[s], E5M2, dz_f[s])
+
+        def quant_t(t):
+            quantize(t_mx[t], E5M2, dz_t[t])
+
+        group_x_slot = {0: 0, 1: 1, 4: 2, 6: 3}
+        quant_x_slot = {1: 0, 2: 1, 5: 2, 7: 3}
+        quant_w_slot = {3: 0, 10: 1}
+        quant_t_slot = {4: 0, 6: 1, 8: 2, 9: 3, 11: 4, 13: 5}
+        dwq_slot = {5: 0, 7: 1, 9: 2, 10: 3}
+
+        turn_g(0)
+        turn_g(1)
+        for s in range(STEPS):
+            if s >= 1:
+                add(s - 1, nc.gpsimd)
+            products(s)
+            if s >= 3 and s % 2 == 1:
+                group_tokens((s - 3) // 2, 0)
+                group_tokens((s - 3) // 2, 1)
+            if s in group_x_slot:
+                group_x(group_x_slot[s])
+            if s in (1, 2):
+                turn_w(s - 1)
+            if s == 2:
+                group_w(0)
+                group_w(1)
+            if s in dwq_slot:
+                for m in range(4):
+                    dw_pass(0, m, dwq_slot[s], "acc%d" % m)
+            if s == 10:
+                for m in range(4):
+                    dw_out(0, m)
+            if 11 <= s <= 13:
+                for j in range(2):
+                    dx_tile(s - 3, j, "acc%d" % ((2 * s + j) % 4))
+            if s == 14:
+                dx_tile(11, 0, "acc3")
+                for q in range(2):
+                    for m in range(3):
+                        dw_pass(1, m, q, "acc%d" % m)
+                dx_tile(11, 1, "acc3")
+            if s == 15:
+                for r in (12, 13):
+                    dx_tile(r, 0, "fwd0")
+                    dx_tile(r, 1, "acc3")
+            if s >= 1:
+                turn_back(s - 1)
+            if s + 2 < STEPS:
+                turn_g(s + 2)
+            if s in quant_x_slot:
+                quantize(x_mx[quant_x_slot[s]], E4M3, x_t[quant_x_slot[s]])
+            if s in quant_w_slot:
+                quantize(w_mx[quant_w_slot[s]], E4M3, w_t[quant_w_slot[s]])
+            if s in quant_t_slot:
+                quant_t(quant_t_slot[s])
+            if s == 14:
+                quant_f(13)
+            if 2 <= s <= 14:
+                quant_f(s - 2)
+
+        add(15, nc.vector)
+        for q in range(2):
+            dw_pass(1, 3, q, "fwd1")
+        quant_f(14)
+        quant_t(6)
+        turn_back(15)
+        quant_f(15)
+        group_tokens(7, 0)
+        group_tokens(7, 1, "vector")
+        for m in range(4):
+            dw_pass(1, m, 2, None)
+        dx_tile(14, 0, "fwd0")
+        dx_tile(14, 1, "acc3")
+        quant_t(7)
+        for m in range(4):
+            dw_pass(1, m, 3, None)
+        dw_out(1, 0, "vector")
+        dw_out(1, 1)
+        dx_tile(15, 0, "fwd0", "vector")
+        dx_tile(15, 1, "acc3")
+        dw_out(1, 2, "vector")
+        dw_out(1, 3)

@@ -19,6 +19,8 @@ SEQS = 4
 L = 512
 D = 512
 STEPS = 16
+VECTOR_SHARE = 192
+HELD_BACK = 32
 FLOPS = 2 * 2 * (SEQS * L) * (2 * D) * D
 
 
@@ -34,7 +36,7 @@ def tile_retention_pa_v_kernel(tc, X, W_Q, W_K, grad_0, grad_1, out_0, out_1, ou
     with ExitStack() as ctx:
         keep = ctx.enter_context(tc.tile_pool(name="keep", bufs=1))
         ring = ctx.enter_context(tc.tile_pool(name="ring", bufs=2))
-        outs = ctx.enter_context(tc.tile_pool(name="outs", bufs=4))
+        outs = ctx.enter_context(tc.tile_pool(name="outs", bufs=10))
         psum = ctx.enter_context(tc.psum_pool(name="psum", bufs=1))
         ctx.enter_context(tc.manual_schedule())
 
@@ -129,27 +131,29 @@ def tile_retention_pa_v_kernel(tc, X, W_Q, W_K, grad_0, grad_1, out_0, out_1, ou
                 for h in range(2):
                     nc.tensor.transpose(g_ps[s][:, h, j, :], words[:, 256 * j + h : 256 * (j + 1) : 2], ident[:])
 
-        def products(s):
+        def product(s, e, tokens=slice(0, 256)):
             tab = table[s % 2]
             pairs = g_ps[s][:].rearrange("p h j r -> p (h j r)").bitcast(BF16).rearrange("p (h n e) -> p n h e", h=2, e=2)
             if s < 8:
-                rows = {0: tab[:, 1:3], 1: tab[:, 0:2]}
+                rows = tab[:, 1:3] if e == 0 else tab[:, 0:2]
             else:
-                rows = {0: tab[:, 1::-1], 1: tab[:, 2:0:-1]}
-            prod[s] = {}
-            for e in (1, 0):
-                prod[s][e] = ring.tile([P, 256, 2, 2], F32, name="prod%d" % e, tag="prod%d" % e)
-                nc.vector.tensor_tensor(
-                    out=prod[s][e][:],
-                    in0=pairs[:, :, :, e : e + 1].to_broadcast([P, 256, 2, 2]),
-                    in1=rows[e].rearrange("p o n h -> p n h o"),
-                    op=ALU.mult,
-                )
+                rows = tab[:, 1::-1] if e == 0 else tab[:, 2:0:-1]
+            if (s, e) not in prod:
+                prod[s, e] = ring.tile([P, 256, 2, 2], F32, name="prod%d" % e, tag="prod%d" % e)
+            nc.vector.tensor_tensor(
+                out=prod[s, e][:, tokens],
+                in0=pairs[:, tokens, :, e : e + 1].to_broadcast([P, tokens.stop - tokens.start, 2, 2]),
+                in1=rows.rearrange("p o n h -> p n h o")[:, tokens],
+                op=ALU.mult,
+            )
 
-        def add(s, engine):
-            dz_f[s] = ring.tile([P, 1024], BF16, name="dz_f", tag="dz_f", align_bytes=64)
+        def add(s, engine, cols):
+            if s not in dz_f:
+                dz_f[s] = ring.tile([P, 1024], BF16, name="dz_f", tag="dz_f", align_bytes=64)
             flat = "p n h o -> p (n h o)"
-            engine.tensor_tensor(out=dz_f[s][:], in0=prod[s][0][:].rearrange(flat), in1=prod[s][1][:].rearrange(flat), op=ALU.add)
+            engine.tensor_tensor(
+                out=dz_f[s][:, cols], in0=prod[s, 0][:].rearrange(flat)[:, cols], in1=prod[s, 1][:].rearrange(flat)[:, cols], op=ALU.add
+            )
 
         def turn_back(s):
             t = s // 2
@@ -167,11 +171,9 @@ def tile_retention_pa_v_kernel(tc, X, W_Q, W_K, grad_0, grad_1, out_0, out_1, ou
                 nc.vector.tensor_copy(out=out, in_=in_)
 
         def group_tokens(t, h, engine="scalar"):
-            if h == 0:
-                dz_t[t] = ring.tile([P, 4 * D], BF16, name="dz_t", tag="dz_t", align_bytes=64)
-            src = back_ps[t][h][:].rearrange("p j r -> p (j r)").bitcast(BF16).rearrange("p (j r e) -> p r e j", j=4, e=2)
-            dst = dz_t[t][:].rearrange("p (r h e j) -> p h r e j", h=2, e=2, j=4)[:, h]
-            copy_on(engine, dst, src)
+            dz_t[t, h] = ring.tile([P, 2 * D], BF16, name="dz_t%d" % h, tag="dz_t%d" % h, align_bytes=64)
+            src = back_ps[t][h][:].rearrange("p j r -> p (j r)").bitcast(BF16).rearrange("p (j c) -> p c j", j=4)
+            copy_on(engine, dz_t[t, h][:].rearrange("p (c j) -> p c j", j=4), src)
 
         def group_x(q):
             x_t[q] = ring.tile([P, 4 * D], BF16, name="x_t", tag="x_t", align_bytes=64)
@@ -204,17 +206,17 @@ def tile_retention_pa_v_kernel(tc, X, W_Q, W_K, grad_0, grad_1, out_0, out_1, ou
                 stop=stop,
             )
 
-        dx_sb, dw_ps = {}, {}
+        dx_ps, dw_ps = {}, {}
 
-        def dx_tile(s, j, tag, engine="scalar"):
-            acc = bank(tag, [P, D])
+        def dx_mul(s, j, tag):
+            dx_ps[s, j] = bank(tag, [P, D])
             for w in range(2):
-                mx_pass(acc, f_mx[s - 8 + 8 * w], E5M2, slice(P * j, P * (j + 1)), w_mx[w], E4M3, w == 0, w == 1)
-            if j == 0:
-                dx_sb[s] = outs.tile([P, 2, D], F32, name="dx_sb", tag="dx_sb")
-            copy_on(engine, dx_sb[s][:, j, :], acc[:])
-            if j == 1:
-                nc.sync.dma_start(out=dx_hbm[(s // 2) % SEQS][:, 2 * (s % 2) : 2 * (s % 2) + 2, :], in_=dx_sb[s][:])
+                mx_pass(dx_ps[s, j], f_mx[s - 8 + 8 * w], E5M2, slice(P * j, P * (j + 1)), w_mx[w], E4M3, w == 0, w == 1)
+
+        def dx_out(s, j, engine="scalar"):
+            dx_sb = outs.tile([P, D], F32, name="out_sb", tag="out_sb")
+            copy_on(engine, dx_sb[:], dx_ps[s, j][:])
+            nc.sync.dma_start(out=dx_hbm[(s // 2) % SEQS][:, 2 * (s % 2) + j, :], in_=dx_sb[:])
 
         def dw_pass(w, m, q, tag):
             if q == 0:
@@ -222,29 +224,42 @@ def tile_retention_pa_v_kernel(tc, X, W_Q, W_K, grad_0, grad_1, out_0, out_1, ou
             mx_pass(dw_ps[w, m], x_mx[q], E4M3, slice(P * m, P * (m + 1)), t_mx[SEQS * w + q], E5M2, q == 0, q == SEQS - 1)
 
         def dw_out(w, m, engine="scalar"):
-            dw_sb = outs.tile([P, D], F32, name="dw_sb", tag="dw_sb")
-            copy_on(engine, dw_sb[:], dw_ps[w, m][:])
+            dw_sb = outs.tile([P, D], F32, name="out_sb", tag="out_sb")
+            copy_on(
+                engine,
+                dw_sb[:].rearrange("p (r h e) -> p r h e", h=2, e=2),
+                dw_ps[w, m][:].rearrange("p (h r e) -> p r h e", h=2, e=2),
+            )
             nc.sync.dma_start(out=dw_hbm[w][P * m : P * (m + 1), :], in_=dw_sb[:])
+
+        def quant_part(pair, part, width, src):
+            cols = slice(part * width, (part + 1) * width)
+            nc.vector.quantize_mx(out=pair[0][:, cols].bitcast(E5M2), scales=pair[1][:, cols], in_=src)
 
         def quant_f(s):
             quantize(f_mx[s], E5M2, dz_f[s])
 
-        def quant_t(t):
-            quantize(t_mx[t], E5M2, dz_t[t])
+        def quant_t(t, halves=(0, 1)):
+            for h in halves:
+                quant_part(t_mx[t], h, 256, dz_t[t, h][:])
 
         group_x_slot = {0: 0, 1: 1, 4: 2, 6: 3}
-        quant_x_slot = {1: 0, 2: 1, 5: 2, 7: 3}
-        quant_w_slot = {3: 0, 10: 1}
-        quant_t_slot = {4: 0, 6: 1, 8: 2, 9: 3, 11: 4, 13: 5}
+        quant_x_slot = {2: 0, 3: 1, 5: 2, 7: 3}
+        quant_t_slot = {4: 0, 6: 1, 8: 2, 9: 3, 12: 4, 13: 5}
         dwq_slot = {5: 0, 7: 1, 9: 2, 10: 3}
+        pool_cols = slice(0, 1024 - VECTOR_SHARE)
+        vector_cols = slice(1024 - VECTOR_SHARE, 1024)
+        all_cols = slice(0, 1024)
 
         turn_g(0)
         turn_g(1)
         for s in range(STEPS):
             if s >= 1:
-                add(s - 1, nc.gpsimd)
-            products(s)
-            if s >= 3 and s % 2 == 1:
+                add(s - 1, nc.gpsimd, pool_cols if s >= 2 else all_cols)
+            product(s, 1)
+            held = 2 * HELD_BACK if s == 14 else 0
+            product(s, 0, slice(held, 256))
+            if s >= 3 and s % 2 == 1 and s < 15:
                 group_tokens((s - 3) // 2, 0)
                 group_tokens((s - 3) // 2, 1)
             if s in group_x_slot:
@@ -260,53 +275,72 @@ def tile_retention_pa_v_kernel(tc, X, W_Q, W_K, grad_0, grad_1, out_0, out_1, ou
             if s == 10:
                 for m in range(4):
                     dw_out(0, m)
-            if 11 <= s <= 13:
+            if 11 <= s <= 14:
                 for j in range(2):
-                    dx_tile(s - 3, j, "acc%d" % ((2 * s + j) % 4))
+                    dx_mul(s - 3, j, "acc%d" % (j + 2 * (s == 12)))
+                    dx_out(s - 3, j)
+            if s in (13, 14):
+                for m in (2, 3):
+                    dw_pass(1, m, s - 13, "acc%d" % m)
             if s == 14:
-                dx_tile(11, 0, "acc3")
-                for q in range(2):
-                    for m in range(3):
-                        dw_pass(1, m, q, "acc%d" % m)
-                dx_tile(11, 1, "acc3")
+                dx_mul(12, 0, "acc0")
+                dx_out(12, 0)
             if s == 15:
-                for r in (12, 13):
-                    dx_tile(r, 0, "fwd0")
-                    dx_tile(r, 1, "acc3")
+                dx_mul(12, 1, "acc1")
+                dx_mul(13, 0, "fwd0")
+                group_tokens(6, 0)
+                dx_out(12, 1)
+                dx_out(13, 0)
+                group_tokens(6, 1)
+                for m in (0, 1):
+                    for q in (0, 1):
+                        dw_pass(1, m, q, "acc%d" % m)
+                dx_mul(13, 1, "fwd0")
+                dx_out(13, 1)
+            if s >= 2:
+                add(s - 1, nc.vector, vector_cols)
             if s >= 1:
                 turn_back(s - 1)
             if s + 2 < STEPS:
                 turn_g(s + 2)
             if s in quant_x_slot:
                 quantize(x_mx[quant_x_slot[s]], E4M3, x_t[quant_x_slot[s]])
-            if s in quant_w_slot:
-                quantize(w_mx[quant_w_slot[s]], E4M3, w_t[quant_w_slot[s]])
-            if s in quant_t_slot:
+            if s == 10:
+                for w in range(2):
+                    quantize(w_mx[w], E4M3, w_t[w])
+            if s == 13:
+                quant_t(5, (0,))
+                quant_f(12)
+                quant_t(5, (1,))
+            elif s in quant_t_slot:
                 quant_t(quant_t_slot[s])
-            if s == 14:
-                quant_f(13)
-            if 2 <= s <= 14:
+            if 2 <= s <= 13:
                 quant_f(s - 2)
+            if s == 14:
+                product(14, 0, slice(HELD_BACK, 2 * HELD_BACK))
+                quant_f(13)
+                product(14, 0, slice(0, HELD_BACK))
 
-        add(15, nc.vector)
-        for q in range(2):
-            dw_pass(1, 3, q, "fwd1")
+        quant_t(6, (0,))
         quant_f(14)
-        quant_t(6)
+        add(15, nc.vector, all_cols)
+        dx_mul(14, 0, "fwd1")
+        dx_out(14, 0)
         turn_back(15)
+        quant_t(6, (1,))
         quant_f(15)
         group_tokens(7, 0)
         group_tokens(7, 1, "vector")
-        for m in range(4):
-            dw_pass(1, m, 2, None)
-        dx_tile(14, 0, "fwd0")
-        dx_tile(14, 1, "acc3")
+        dx_mul(14, 1, "fwd0")
+        dx_out(14, 1)
+        dx_mul(15, 0, "fwd1")
+        dx_out(15, 0)
+        dw_pass(1, 0, 2, None)
+        dx_mul(15, 1, "fwd0")
+        dx_out(15, 1)
         quant_t(7)
         for m in range(4):
+            if m > 0:
+                dw_pass(1, m, 2, None)
             dw_pass(1, m, 3, None)
-        dw_out(1, 0, "vector")
-        dw_out(1, 1)
-        dx_tile(15, 0, "fwd0", "vector")
-        dx_tile(15, 1, "acc3")
-        dw_out(1, 2, "vector")
-        dw_out(1, 3)
+            dw_out(1, m, "vector" if m % 2 == 0 else "scalar")

@@ -13,13 +13,14 @@ E4M3 = mybir.dt.float8_e4m3fn_x4
 E5M2 = mybir.dt.float8_e5m2_x4
 ALU = mybir.AluOpType
 SIN = mybir.ActivationFunctionType.Sin
+ABS = mybir.ActivationFunctionType.Abs
 
 P = 128
 SEQS = 4
 L = 512
 D = 512
 STEPS = 16
-VECTOR_SHARE = 192
+VECTOR_SHARE = 224
 HELD_BACK = 32
 FLOPS = 2 * 2 * (SEQS * L) * (2 * D) * D
 
@@ -78,7 +79,7 @@ def tile_retention_pa_v_kernel(tc, X, W_Q, W_K, grad_0, grad_1, out_0, out_1, ou
         ident = keep.tile([P, P], F32, name="ident")
         make_identity(nc, ident[:])
         pos = keep.tile([P, L], F32, name="pos")
-        nc.gpsimd.iota(pos[:], pattern=[[1, 4], [4, P]], base=0, channel_multiplier=0, allow_small_or_imprecise_dtypes=True)
+        nc.gpsimd.iota(pos[:, :P], pattern=[[4, P]], base=0, channel_multiplier=0, allow_small_or_imprecise_dtypes=True)
 
         ratio = 10000.0 ** (-1.0 / 255.0)
         one = keep.tile([P, 1], F32, name="one")
@@ -94,26 +95,31 @@ def tile_retention_pa_v_kernel(tc, X, W_Q, W_K, grad_0, grad_1, out_0, out_1, ou
         turns_ps = bank("acc0", [P, 2, P])
         for h in range(2):
             nc.tensor.transpose(turns_ps[:, h, :], turns_row[:, h::2], ident[:])
+        for j in range(1, 4):
+            nc.vector.tensor_scalar(out=pos[:, P * j : P * (j + 1)], in0=pos[:, :P], scalar1=float(j), scalar2=None, op0=ALU.add)
         turns = keep.tile([P, 2], F32, name="turns")
         nc.vector.tensor_copy(out=turns[:], in_=turns_ps[:, :, 0])
 
-        whole = [keep.tile([P, L], I32, name="whole%d" % h) for h in range(2)]
-        for h in range(2):
-            nc.vector.tensor_scalar(out=whole[h][:], in0=pos[:], scalar1=turns[:, h : h + 1], scalar2=None, op0=ALU.mult)
         table = []
         for a in range(2):
             cols = slice(256 * a, 256 * (a + 1))
+            whole = keep.tile([P, 2, 256], I32, name="whole%d" % a)
             frac = keep.tile([P, 2, 256], F32, name="frac%d" % a)
             size = keep.tile([P, 2, 256], F32, name="size%d" % a)
             for h in range(2):
+                nc.vector.tensor_scalar(out=whole[:, h, :], in0=pos[:, cols], scalar1=turns[:, h : h + 1], scalar2=None, op0=ALU.mult)
+            for h in range(2):
                 nc.vector.scalar_tensor_tensor(
-                    out=frac[:, h, :], in0=pos[:, cols], scalar=turns[:, h : h + 1], in1=whole[h][:, cols], op0=ALU.mult, op1=ALU.subtract
+                    out=frac[:, h, :], in0=pos[:, cols], scalar=turns[:, h : h + 1], in1=whole[:, h, :], op0=ALU.mult, op1=ALU.subtract
                 )
-            nc.vector.scalar_tensor_tensor(out=size[:], in0=frac[:], scalar=-1.0, in1=frac[:], op0=ALU.mult, op1=ALU.max)
+            if a == 0:
+                nc.vector.scalar_tensor_tensor(out=size[:], in0=frac[:], scalar=-1.0, in1=frac[:], op0=ALU.mult, op1=ALU.max)
             tab = keep.tile([P, 3, 256, 2], F32, name="table%d" % a)
             frac_nh = frac[:].rearrange("p h n -> p n h")
             size_nh = size[:].rearrange("p h n -> p n h")
             nc.scalar.activation(out=tab[:, 0], in_=frac_nh, func=SIN, scale=2 * math.pi)
+            if a == 1:
+                nc.scalar.activation(out=size[:], in_=frac[:], func=ABS)
             nc.scalar.activation(out=tab[:, 1], in_=size_nh, func=SIN, scale=-2 * math.pi, bias=math.pi / 2)
             nc.scalar.activation(out=tab[:, 2], in_=frac_nh, func=SIN, scale=-2 * math.pi)
             table.append(tab)
@@ -255,7 +261,7 @@ def tile_retention_pa_v_kernel(tc, X, W_Q, W_K, grad_0, grad_1, out_0, out_1, ou
         turn_g(1)
         for s in range(STEPS):
             if s >= 1:
-                add(s - 1, nc.gpsimd, pool_cols if s >= 2 else all_cols)
+                add(s - 1, nc.gpsimd, pool_cols)
             product(s, 1)
             held = 2 * HELD_BACK if s == 14 else 0
             product(s, 0, slice(held, 256))
@@ -297,9 +303,9 @@ def tile_retention_pa_v_kernel(tc, X, W_Q, W_K, grad_0, grad_1, out_0, out_1, ou
                         dw_pass(1, m, q, "acc%d" % m)
                 dx_mul(13, 1, "fwd0")
                 dx_out(13, 1)
-            if s >= 2:
-                add(s - 1, nc.vector, vector_cols)
             if s >= 1:
+                add(s - 1, nc.vector, vector_cols)
+            if 1 <= s <= 14:
                 turn_back(s - 1)
             if s + 2 < STEPS:
                 turn_g(s + 2)
@@ -326,9 +332,10 @@ def tile_retention_pa_v_kernel(tc, X, W_Q, W_K, grad_0, grad_1, out_0, out_1, ou
         add(15, nc.vector, all_cols)
         dx_mul(14, 0, "fwd1")
         dx_out(14, 0)
+        turn_back(14)
         turn_back(15)
-        quant_t(6, (1,))
         quant_f(15)
+        quant_t(6, (1,))
         group_tokens(7, 0)
         group_tokens(7, 1, "vector")
         dx_mul(14, 1, "fwd0")
@@ -336,11 +343,11 @@ def tile_retention_pa_v_kernel(tc, X, W_Q, W_K, grad_0, grad_1, out_0, out_1, ou
         dx_mul(15, 0, "fwd1")
         dx_out(15, 0)
         dw_pass(1, 0, 2, None)
-        dx_mul(15, 1, "fwd0")
-        dx_out(15, 1)
         quant_t(7)
+        dx_mul(15, 1, "back0")
+        dx_out(15, 1, "vector")
         for m in range(4):
             if m > 0:
                 dw_pass(1, m, 2, None)
             dw_pass(1, m, 3, None)
-            dw_out(1, m, "vector" if m % 2 == 0 else "scalar")
+            dw_out(1, m, "scalar" if m % 2 == 0 else "vector")

@@ -2,7 +2,6 @@ import math
 from contextlib import ExitStack
 
 import concourse.mybir as mybir
-from concourse.masks import make_identity
 
 F32 = mybir.dt.float32
 BF16 = mybir.dt.bfloat16
@@ -76,29 +75,27 @@ def tile_retention_pa_v_kernel(tc, X, W_Q, W_K, grad_0, grad_1, out_0, out_1, ou
         for s in range(8, STEPS):
             load_g(s)
 
-        ident = keep.tile([P, P], F32, name="ident")
-        make_identity(nc, ident[:])
+        pair = keep.tile([P, 2], F32, name="pair")
+        nc.gpsimd.iota(pair[:], pattern=[[1, 2]], base=0, channel_multiplier=2, allow_small_or_imprecise_dtypes=True)
         pos = keep.tile([P, L], F32, name="pos")
-        nc.gpsimd.iota(pos[:, :P], pattern=[[4, P]], base=0, channel_multiplier=0, allow_small_or_imprecise_dtypes=True)
+        nc.gpsimd.iota(pos[:], pattern=[[1, 4], [4, P]], base=0, channel_multiplier=0, allow_small_or_imprecise_dtypes=True)
 
-        ratio = 10000.0 ** (-1.0 / 255.0)
-        one = keep.tile([P, 1], F32, name="one")
-        nc.vector.memset(one[:], 1.0)
-        turns_row = keep.tile([P, 256], F32, name="turns_row")
-        for b in range(8):
-            nc.vector.tensor_scalar(out=turns_row[:, b : b + 1], in0=one[:], scalar1=ratio**b / (2 * math.pi), scalar2=None, op0=ALU.mult)
-        for have, copies in ((8, 8), (64, 4)):
-            for a in range(1, copies):
-                nc.vector.tensor_scalar(
-                    out=turns_row[:, a * have : (a + 1) * have], in0=turns_row[:, :have], scalar1=ratio ** (a * have), scalar2=None, op0=ALU.mult
-                )
-        turns_ps = bank("acc0", [P, 2, P])
-        for h in range(2):
-            nc.tensor.transpose(turns_ps[:, h, :], turns_row[:, h::2], ident[:])
-        for j in range(1, 4):
-            nc.vector.tensor_scalar(out=pos[:, P * j : P * (j + 1)], in0=pos[:, :P], scalar1=float(j), scalar2=None, op0=ALU.add)
+        short_step = 65793.0 / 2.0**24
+        left_over = (1.0 / 255.0 - short_step) * math.log(10000.0)
+        base = keep.tile([P, 2], F32, name="base")
+        nc.vector.memset(base[:], 10000.0)
+        power = keep.tile([P, 2], F32, name="power")
+        nc.vector.tensor_scalar(out=power[:], in0=pair[:], scalar1=-short_step, scalar2=None, op0=ALU.mult)
+        per_turn = keep.tile([P, 2], F32, name="per_turn")
+        nc.vector.tensor_scalar(
+            out=per_turn[:], in0=pair[:], scalar1=-left_over / (2 * math.pi), scalar2=1.0 / (2 * math.pi), op0=ALU.mult, op1=ALU.add
+        )
+        speed = keep.tile([P, 2], F32, name="speed")
+        nc.gpsimd.tensor_tensor(out=speed[:], in0=base[:], in1=power[:], op=ALU.pow)
         turns = keep.tile([P, 2], F32, name="turns")
-        nc.vector.tensor_copy(out=turns[:], in_=turns_ps[:, :, 0])
+        nc.vector.tensor_tensor(out=turns[:], in0=speed[:], in1=per_turn[:], op=ALU.mult)
+        ident = keep.tile([P, P], F32, name="ident")
+        nc.vector.tensor_scalar(out=ident[:], in0=pos[:, :P], scalar1=0.5, scalar2=pair[:, 0:1], op0=ALU.mult, op1=ALU.is_equal)
 
         table = []
         for a in range(2):
@@ -117,14 +114,14 @@ def tile_retention_pa_v_kernel(tc, X, W_Q, W_K, grad_0, grad_1, out_0, out_1, ou
             tab = keep.tile([P, 3, 256, 2], F32, name="table%d" % a)
             frac_nh = frac[:].rearrange("p h n -> p n h")
             size_nh = size[:].rearrange("p h n -> p n h")
-            nc.scalar.activation(out=tab[:, 0], in_=frac_nh, func=SIN, scale=2 * math.pi)
             if a == 1:
                 nc.scalar.activation(out=size[:], in_=frac[:], func=ABS)
+            nc.scalar.activation(out=tab[:, 0], in_=frac_nh, func=SIN, scale=2 * math.pi)
             nc.scalar.activation(out=tab[:, 1], in_=size_nh, func=SIN, scale=-2 * math.pi, bias=math.pi / 2)
             nc.scalar.activation(out=tab[:, 2], in_=frac_nh, func=SIN, scale=-2 * math.pi)
             table.append(tab)
 
-        g_ps, prod, dz_f, back_ps, dz_t, x_t, w_ps, w_t = {}, {}, {}, {}, {}, {}, {}, {}
+        g_ps, prod, dz_f, back_ps, dz_t, x_t, w_t = {}, {}, {}, {}, {}, {}, {}
         f_mx = [mx_pair("f%d" % s, 256) for s in range(STEPS)]
         t_mx = [mx_pair("t%d" % t, D) for t in range(2 * SEQS)]
         x_mx = [mx_pair("x%d" % q, D) for q in range(SEQS)]
@@ -177,9 +174,10 @@ def tile_retention_pa_v_kernel(tc, X, W_Q, W_K, grad_0, grad_1, out_0, out_1, ou
                 nc.vector.tensor_copy(out=out, in_=in_)
 
         def group_tokens(t, h, engine="scalar"):
-            dz_t[t, h] = ring.tile([P, 2 * D], BF16, name="dz_t%d" % h, tag="dz_t%d" % h, align_bytes=64)
+            if h == 0:
+                dz_t[t] = ring.tile([P, 4 * D], BF16, name="dz_t", tag="dz_t", align_bytes=64)
             src = back_ps[t][h][:].rearrange("p j r -> p (j r)").bitcast(BF16).rearrange("p (j c) -> p c j", j=4)
-            copy_on(engine, dz_t[t, h][:].rearrange("p (c j) -> p c j", j=4), src)
+            copy_on(engine, dz_t[t][:, 2 * D * h : 2 * D * (h + 1)].rearrange("p (c j) -> p c j", j=4), src)
 
         def group_x(q):
             x_t[q] = ring.tile([P, 4 * D], BF16, name="x_t", tag="x_t", align_bytes=64)
@@ -188,18 +186,17 @@ def tile_retention_pa_v_kernel(tc, X, W_Q, W_K, grad_0, grad_1, out_0, out_1, ou
                 in_=x_raw[q][:].rearrange("p j (c i) -> p c j i", i=4),
             )
 
-        def turn_w(w):
+        def turn_w(w, b):
             words = w_raw[w][:].rearrange("r a f -> r (a f)").bitcast(F32)
-            w_ps[w] = [bank("acc%d" % (2 * w + b), [P, 2, 2, P]) for b in range(2)]
-            for a in range(4):
+            w_ps = bank("acc%d" % (2 * w + b), [P, 2, 2, P])
+            for a in range(2):
                 for h in range(2):
-                    nc.tensor.transpose(w_ps[w][a // 2][:, a % 2, h, :], words[:, 256 * a + h : 256 * (a + 1) : 2], ident[:])
-
-        def group_w(w):
-            w_t[w] = ring.tile([P, 4 * D], BF16, name="w_t", tag="w_t", align_bytes=64)
+                    first = 256 * (2 * b + a)
+                    nc.tensor.transpose(w_ps[:, a, h, :], words[:, first + h : first + 256 : 2], ident[:])
+            if b == 0:
+                w_t[w] = ring.tile([P, 4 * D], BF16, name="w_t", tag="w_t", align_bytes=64)
             dst = w_t[w][:].bitcast(F32).rearrange("p (a r h) -> p a r h", a=4, h=2)
-            for b in range(2):
-                nc.scalar.copy(out=dst[:, 2 * b : 2 * b + 2], in_=w_ps[w][b][:].rearrange("p a h r -> p a r h"))
+            nc.scalar.copy(out=dst[:, 2 * b : 2 * b + 2], in_=w_ps[:].rearrange("p a h r -> p a r h"))
 
         def mx_pass(acc, still, still_fmt, cols, moving, moving_fmt, start, stop):
             nc.tensor.matmul_mx(
@@ -238,16 +235,17 @@ def tile_retention_pa_v_kernel(tc, X, W_Q, W_K, grad_0, grad_1, out_0, out_1, ou
             )
             nc.sync.dma_start(out=dw_hbm[w][P * m : P * (m + 1), :], in_=dw_sb[:])
 
-        def quant_part(pair, part, width, src):
-            cols = slice(part * width, (part + 1) * width)
-            nc.vector.quantize_mx(out=pair[0][:, cols].bitcast(E5M2), scales=pair[1][:, cols], in_=src)
-
         def quant_f(s):
             quantize(f_mx[s], E5M2, dz_f[s])
 
-        def quant_t(t, halves=(0, 1)):
-            for h in halves:
-                quant_part(t_mx[t], h, 256, dz_t[t, h][:])
+        def quant_t(t):
+            quantize(t_mx[t], E5M2, dz_t[t])
+
+        def quant_t_half(t, h):
+            cols = slice(256 * h, 256 * (h + 1))
+            nc.vector.quantize_mx(
+                out=t_mx[t][0][:, cols].bitcast(E5M2), scales=t_mx[t][1][:, cols], in_=dz_t[t][:, 2 * D * h : 2 * D * (h + 1)]
+            )
 
         group_x_slot = {0: 0, 1: 1, 4: 2, 6: 3}
         quant_x_slot = {2: 0, 3: 1, 5: 2, 7: 3}
@@ -270,11 +268,8 @@ def tile_retention_pa_v_kernel(tc, X, W_Q, W_K, grad_0, grad_1, out_0, out_1, ou
                 group_tokens((s - 3) // 2, 1)
             if s in group_x_slot:
                 group_x(group_x_slot[s])
-            if s in (1, 2):
-                turn_w(s - 1)
-            if s == 2:
-                group_w(0)
-                group_w(1)
+            if 1 <= s <= 4:
+                turn_w((s - 1) // 2, (s - 1) % 2)
             if s in dwq_slot:
                 for m in range(4):
                     dw_pass(0, m, dwq_slot[s], "acc%d" % m)
@@ -315,9 +310,9 @@ def tile_retention_pa_v_kernel(tc, X, W_Q, W_K, grad_0, grad_1, out_0, out_1, ou
                 for w in range(2):
                     quantize(w_mx[w], E4M3, w_t[w])
             if s == 13:
-                quant_t(5, (0,))
+                quant_t_half(5, 0)
                 quant_f(12)
-                quant_t(5, (1,))
+                quant_t_half(5, 1)
             elif s in quant_t_slot:
                 quant_t(quant_t_slot[s])
             if 2 <= s <= 13:
@@ -327,7 +322,7 @@ def tile_retention_pa_v_kernel(tc, X, W_Q, W_K, grad_0, grad_1, out_0, out_1, ou
                 quant_f(13)
                 product(14, 0, slice(0, HELD_BACK))
 
-        quant_t(6, (0,))
+        quant_t_half(6, 0)
         quant_f(14)
         add(15, nc.vector, all_cols)
         dx_mul(14, 0, "fwd1")
@@ -335,7 +330,7 @@ def tile_retention_pa_v_kernel(tc, X, W_Q, W_K, grad_0, grad_1, out_0, out_1, ou
         turn_back(14)
         turn_back(15)
         quant_f(15)
-        quant_t(6, (1,))
+        quant_t_half(6, 1)
         group_tokens(7, 0)
         group_tokens(7, 1, "vector")
         dx_mul(14, 1, "fwd0")
@@ -343,7 +338,8 @@ def tile_retention_pa_v_kernel(tc, X, W_Q, W_K, grad_0, grad_1, out_0, out_1, ou
         dx_mul(15, 0, "fwd1")
         dx_out(15, 0)
         dw_pass(1, 0, 2, None)
-        quant_t(7)
+        quant_t_half(7, 0)
+        quant_t_half(7, 1)
         dx_mul(15, 1, "back0")
         dx_out(15, 1, "vector")
         for m in range(4):

@@ -19,7 +19,7 @@ SEQS = 4
 L = 512
 D = 512
 STEPS = 16
-VECTOR_SHARE = 224
+VECTOR_SHARE = 208
 HELD_BACK = 32
 FLOPS = 2 * 2 * (SEQS * L) * (2 * D) * D
 
@@ -69,16 +69,15 @@ def tile_retention_pa_v_kernel(tc, X, W_Q, W_K, grad_0, grad_1, out_0, out_1, ou
             load_g(2 * q)
             load_g(2 * q + 1)
             load_x(q)
-            if q == 1:
-                load_w(0)
-                load_w(1)
+            if q < 2:
+                load_w(q)
         for s in range(8, STEPS):
             load_g(s)
 
         pair = keep.tile([P, 2], F32, name="pair")
         nc.gpsimd.iota(pair[:], pattern=[[1, 2]], base=0, channel_multiplier=2, allow_small_or_imprecise_dtypes=True)
         pos = keep.tile([P, L], F32, name="pos")
-        nc.gpsimd.iota(pos[:], pattern=[[1, 4], [4, P]], base=0, channel_multiplier=0, allow_small_or_imprecise_dtypes=True)
+        nc.gpsimd.iota(pos[:, :256], pattern=[[1, 2], [4, P]], base=0, channel_multiplier=0, allow_small_or_imprecise_dtypes=True)
 
         short_step = 65793.0 / 2.0**24
         left_over = (1.0 / 255.0 - short_step) * math.log(10000.0)
@@ -96,6 +95,8 @@ def tile_retention_pa_v_kernel(tc, X, W_Q, W_K, grad_0, grad_1, out_0, out_1, ou
         nc.vector.tensor_tensor(out=turns[:], in0=speed[:], in1=per_turn[:], op=ALU.mult)
         ident = keep.tile([P, P], F32, name="ident")
         nc.vector.tensor_scalar(out=ident[:], in0=pos[:, :P], scalar1=0.5, scalar2=pair[:, 0:1], op0=ALU.mult, op1=ALU.is_equal)
+
+        nc.vector.tensor_scalar(out=pos[:, 256:], in0=pos[:, :256], scalar1=2.0, scalar2=None, op0=ALU.add)
 
         table = []
         for a in range(2):
@@ -136,7 +137,7 @@ def tile_retention_pa_v_kernel(tc, X, W_Q, W_K, grad_0, grad_1, out_0, out_1, ou
 
         def product(s, e, tokens=slice(0, 256)):
             tab = table[s % 2]
-            pairs = g_ps[s][:].rearrange("p h j r -> p (h j r)").bitcast(BF16).rearrange("p (h n e) -> p n h e", h=2, e=2)
+            pairs = g_ps[s][:].rearrange("p h j r -> p (h j r)").bitcast(BF16).rearrange("p (h n e) -> p n e h", h=2, e=2)
             if s < 8:
                 rows = tab[:, 1:3] if e == 0 else tab[:, 0:2]
             else:
@@ -145,15 +146,15 @@ def tile_retention_pa_v_kernel(tc, X, W_Q, W_K, grad_0, grad_1, out_0, out_1, ou
                 prod[s, e] = ring.tile([P, 256, 2, 2], F32, name="prod%d" % e, tag="prod%d" % e)
             nc.vector.tensor_tensor(
                 out=prod[s, e][:, tokens],
-                in0=pairs[:, tokens, :, e : e + 1].to_broadcast([P, tokens.stop - tokens.start, 2, 2]),
-                in1=rows.rearrange("p o n h -> p n h o")[:, tokens],
+                in0=pairs[:, tokens, e : e + 1, :].to_broadcast([P, tokens.stop - tokens.start, 2, 2]),
+                in1=rows.rearrange("p o n h -> p n o h")[:, tokens],
                 op=ALU.mult,
             )
 
         def add(s, engine, cols):
             if s not in dz_f:
                 dz_f[s] = ring.tile([P, 1024], BF16, name="dz_f", tag="dz_f", align_bytes=64)
-            flat = "p n h o -> p (n h o)"
+            flat = "p n o h -> p (n o h)"
             engine.tensor_tensor(
                 out=dz_f[s][:, cols], in0=prod[s, 0][:].rearrange(flat)[:, cols], in1=prod[s, 1][:].rearrange(flat)[:, cols], op=ALU.add
             )
@@ -195,8 +196,9 @@ def tile_retention_pa_v_kernel(tc, X, W_Q, W_K, grad_0, grad_1, out_0, out_1, ou
                     nc.tensor.transpose(w_ps[:, a, h, :], words[:, first + h : first + 256 : 2], ident[:])
             if b == 0:
                 w_t[w] = ring.tile([P, 4 * D], BF16, name="w_t", tag="w_t", align_bytes=64)
-            dst = w_t[w][:].bitcast(F32).rearrange("p (a r h) -> p a r h", a=4, h=2)
-            nc.scalar.copy(out=dst[:, 2 * b : 2 * b + 2], in_=w_ps[:].rearrange("p a h r -> p a r h"))
+            dst = w_t[w][:].rearrange("p (a r o h) -> p a r o h", a=4, o=2, h=2)
+            src = w_ps[:].rearrange("p a h r -> p (a h r)").bitcast(BF16).rearrange("p (a h r o) -> p a r o h", a=2, h=2, o=2)
+            nc.scalar.copy(out=dst[:, 2 * b : 2 * b + 2], in_=src)
 
         def mx_pass(acc, still, still_fmt, cols, moving, moving_fmt, start, stop):
             nc.tensor.matmul_mx(
@@ -230,8 +232,8 @@ def tile_retention_pa_v_kernel(tc, X, W_Q, W_K, grad_0, grad_1, out_0, out_1, ou
             dw_sb = outs.tile([P, D], F32, name="out_sb", tag="out_sb")
             copy_on(
                 engine,
-                dw_sb[:].rearrange("p (r h e) -> p r h e", h=2, e=2),
-                dw_ps[w, m][:].rearrange("p (h r e) -> p r h e", h=2, e=2),
+                dw_sb[:].rearrange("p (c o) -> p c o", o=2),
+                dw_ps[w, m][:].rearrange("p (o c) -> p c o", o=2),
             )
             nc.sync.dma_start(out=dw_hbm[w][P * m : P * (m + 1), :], in_=dw_sb[:])
 
@@ -247,8 +249,9 @@ def tile_retention_pa_v_kernel(tc, X, W_Q, W_K, grad_0, grad_1, out_0, out_1, ou
                 out=t_mx[t][0][:, cols].bitcast(E5M2), scales=t_mx[t][1][:, cols], in_=dz_t[t][:, 2 * D * h : 2 * D * (h + 1)]
             )
 
-        group_x_slot = {0: 0, 1: 1, 4: 2, 6: 3}
-        quant_x_slot = {2: 0, 3: 1, 5: 2, 7: 3}
+        group_x_slot = {0: 0, 4: 1, 6: 2, 8: 3}
+        quant_x_slot = {2: 0, 5: 1, 7: 2, 9: 3}
+        quant_w_slot = {3: 0, 10: 1}
         quant_t_slot = {4: 0, 6: 1, 8: 2, 9: 3, 12: 4, 13: 5}
         dwq_slot = {5: 0, 7: 1, 9: 2, 10: 3}
         pool_cols = slice(0, 1024 - VECTOR_SHARE)
@@ -268,8 +271,11 @@ def tile_retention_pa_v_kernel(tc, X, W_Q, W_K, grad_0, grad_1, out_0, out_1, ou
                 group_tokens((s - 3) // 2, 1)
             if s in group_x_slot:
                 group_x(group_x_slot[s])
-            if 1 <= s <= 4:
-                turn_w((s - 1) // 2, (s - 1) % 2)
+            if s == 0:
+                turn_w(0, 0)
+                turn_w(0, 1)
+            if s in (1, 2):
+                turn_w(1, s - 1)
             if s in dwq_slot:
                 for m in range(4):
                     dw_pass(0, m, dwq_slot[s], "acc%d" % m)
@@ -300,15 +306,16 @@ def tile_retention_pa_v_kernel(tc, X, W_Q, W_K, grad_0, grad_1, out_0, out_1, ou
                 dx_out(13, 1)
             if s >= 1:
                 add(s - 1, nc.vector, vector_cols)
+            if s < 8:
+                turn_g(s + 2)
             if 1 <= s <= 14:
                 turn_back(s - 1)
-            if s + 2 < STEPS:
+            if 8 <= s < STEPS - 2:
                 turn_g(s + 2)
             if s in quant_x_slot:
                 quantize(x_mx[quant_x_slot[s]], E4M3, x_t[quant_x_slot[s]])
-            if s == 10:
-                for w in range(2):
-                    quantize(w_mx[w], E4M3, w_t[w])
+            if s in quant_w_slot:
+                quantize(w_mx[quant_w_slot[s]], E4M3, w_t[quant_w_slot[s]])
             if s == 13:
                 quant_t_half(5, 0)
                 quant_f(12)

import math
from contextlib import ExitStack

import concourse.mybir as mybir

F32 = mybir.dt.float32
BF16 = mybir.dt.bfloat16
I32 = mybir.dt.int32
U32 = mybir.dt.uint32
U8 = mybir.dt.uint8
E4M3 = mybir.dt.float8_e4m3fn_x4
E5M2 = mybir.dt.float8_e5m2_x4
ALU = mybir.AluOpType
SIN = mybir.ActivationFunctionType.Sin
ABS = mybir.ActivationFunctionType.Abs

P = 128
SEQS = 4
L = 512
D = 512
STEPS = 16
VECTOR_SHARE = 208
HELD_BACK = 32
FLOPS = 2 * 2 * (SEQS * L) * (2 * D) * D


def tile_retention_pa_v_kernel(tc, X, W_Q, W_K, grad_0, grad_1, out_0, out_1, out_2):
    nc = tc.nc
    quad = "b h (p j) f -> (b h) p j f"
    x_hbm = X.rearrange(quad, j=4)
    g_hbm = [grad_0.rearrange(quad, j=4), grad_1.rearrange(quad, j=4)]
    dx_hbm = out_0.rearrange(quad, j=4)
    w_hbm = [W_Q.rearrange("(a r) f -> r a f", r=P), W_K.rearrange("(a r) f -> r a f", r=P)]
    dw_hbm = [out_1, out_2]

    with ExitStack() as ctx:
        keep = ctx.enter_context(tc.tile_pool(name="keep", bufs=1))
        ring = ctx.enter_context(tc.tile_pool(name="ring", bufs=2))
        outs = ctx.enter_context(tc.tile_pool(name="outs", bufs=10))
        psum = ctx.enter_context(tc.psum_pool(name="psum", bufs=1))
        ctx.enter_context(tc.manual_schedule())

        def bank(tag, shape):
            return psum.tile(shape, F32, name=tag, tag=tag)

        def mx_pair(name, width):
            codes = keep.tile([P, width], U32, name=name + "_codes", align_bytes=64)
            scales = keep.tile([P, width], U8, name=name + "_scales", align_bytes=64)
            return codes, scales

        def quantize(pair, fmt, src):
            nc.vector.quantize_mx(out=pair[0][:].bitcast(fmt), scales=pair[1][:], in_=src[:])

        g_raw, x_raw, w_raw = {}, {}, {}

        def load_g(s):
            g_raw[s] = keep.tile([P, 2, D], BF16, name="g_raw%d" % s, align_bytes=64)
            nc.sync.dma_start(out=g_raw[s][:], in_=g_hbm[s // 8][(s // 2) % SEQS][:, 2 * (s % 2) : 2 * (s % 2) + 2, :])

        def load_x(q):
            x_raw[q] = keep.tile([P, 4, D], BF16, name="x_raw%d" % q, align_bytes=64)
            nc.sync.dma_start(out=x_raw[q][:], in_=x_hbm[q])

        def load_w(w):
            w_raw[w] = keep.tile([P, 4, D], BF16, name="w_raw%d" % w, align_bytes=64)
            nc.sync.dma_start(out=w_raw[w][:], in_=w_hbm[w])

        for q in range(SEQS):
            load_g(2 * q)
            load_g(2 * q + 1)
            load_x(q)
            if q < 2:
                load_w(q)
        for s in range(8, STEPS):
            load_g(s)

        pair = keep.tile([P, 2], F32, name="pair")
        nc.gpsimd.iota(pair[:], pattern=[[1, 2]], base=0, channel_multiplier=2, allow_small_or_imprecise_dtypes=True)
        pos = keep.tile([P, L], F32, name="pos")
        nc.gpsimd.iota(pos[:, :256], pattern=[[1, 2], [4, P]], base=0, channel_multiplier=0, allow_small_or_imprecise_dtypes=True)

        short_step = 65793.0 / 2.0**24
        left_over = (1.0 / 255.0 - short_step) * math.log(10000.0)
        base = keep.tile([P, 2], F32, name="base")
        nc.vector.memset(base[:], 10000.0)
        power = keep.tile([P, 2], F32, name="power")
        nc.vector.tensor_scalar(out=power[:], in0=pair[:], scalar1=-short_step, scalar2=None, op0=ALU.mult)
        per_turn = keep.tile([P, 2], F32, name="per_turn")
        nc.vector.tensor_scalar(
            out=per_turn[:], in0=pair[:], scalar1=-left_over / (2 * math.pi), scalar2=1.0 / (2 * math.pi), op0=ALU.mult, op1=ALU.add
        )
        speed = keep.tile([P, 2], F32, name="speed")
        nc.gpsimd.tensor_tensor(out=speed[:], in0=base[:], in1=power[:], op=ALU.pow)
        turns = keep.tile([P, 2], F32, name="turns")
        nc.vector.tensor_tensor(out=turns[:], in0=speed[:], in1=per_turn[:], op=ALU.mult)
        ident = keep.tile([P, P], F32, name="ident")
        nc.vector.tensor_scalar(out=ident[:], in0=pos[:, :P], scalar1=0.5, scalar2=pair[:, 0:1], op0=ALU.mult, op1=ALU.is_equal)

        nc.vector.tensor_scalar(out=pos[:, 256:], in0=pos[:, :256], scalar1=2.0, scalar2=None, op0=ALU.add)

        table = []
        for a in range(2):
            cols = slice(256 * a, 256 * (a + 1))
            whole = keep.tile([P, 2, 256], I32, name="whole%d" % a)
            frac = keep.tile([P, 2, 256], F32, name="frac%d" % a)
            size = keep.tile([P, 2, 256], F32, name="size%d" % a)
            for h in range(2):
                nc.vector.tensor_scalar(out=whole[:, h, :], in0=pos[:, cols], scalar1=turns[:, h : h + 1], scalar2=None, op0=ALU.mult)
            for h in range(2):
                nc.vector.scalar_tensor_tensor(
                    out=frac[:, h, :], in0=pos[:, cols], scalar=turns[:, h : h + 1], in1=whole[:, h, :], op0=ALU.mult, op1=ALU.subtract
                )
            if a == 0:
                nc.vector.scalar_tensor_tensor(out=size[:], in0=frac[:], scalar=-1.0, in1=frac[:], op0=ALU.mult, op1=ALU.max)
            tab = keep.tile([P, 3, 256, 2], F32, name="table%d" % a)
            frac_nh = frac[:].rearrange("p h n -> p n h")
            size_nh = size[:].rearrange("p h n -> p n h")
            if a == 1:
                nc.scalar.activation(out=size[:], in_=frac[:], func=ABS)
            nc.scalar.activation(out=tab[:, 0], in_=frac_nh, func=SIN, scale=2 * math.pi)
            nc.scalar.activation(out=tab[:, 1], in_=size_nh, func=SIN, scale=-2 * math.pi, bias=math.pi / 2)
            nc.scalar.activation(out=tab[:, 2], in_=frac_nh, func=SIN, scale=-2 * math.pi)
            table.append(tab)

        g_ps, prod, dz_f, back_ps, dz_t, x_t, w_t = {}, {}, {}, {}, {}, {}, {}
        f_mx = [mx_pair("f%d" % s, 256) for s in range(STEPS)]
        t_mx = [mx_pair("t%d" % t, D) for t in range(2 * SEQS)]
        x_mx = [mx_pair("x%d" % q, D) for q in range(SEQS)]
        w_mx = [mx_pair("w%d" % w, D) for w in range(2)]

        def turn_g(s):
            g_ps[s] = bank("fwd%d" % (s % 2), [P, 2, 2, P])
            words = g_raw[s][:].rearrange("p j f -> p (j f)").bitcast(F32)
            for j in range(2):
                for h in range(2):
                    nc.tensor.transpose(g_ps[s][:, h, j, :], words[:, 256 * j + h : 256 * (j + 1) : 2], ident[:])

        def product(s, e, tokens=slice(0, 256)):
            tab = table[s % 2]
            pairs = g_ps[s][:].rearrange("p h j r -> p (h j r)").bitcast(BF16).rearrange("p (h n e) -> p n e h", h=2, e=2)
            if s < 8:
                rows = tab[:, 1:3] if e == 0 else tab[:, 0:2]
            else:
                rows = tab[:, 1::-1] if e == 0 else tab[:, 2:0:-1]
            if (s, e) not in prod:
                prod[s, e] = ring.tile([P, 256, 2, 2], F32, name="prod%d" % e, tag="prod%d" % e)
            nc.vector.tensor_tensor(
                out=prod[s, e][:, tokens],
                in0=pairs[:, tokens, e : e + 1, :].to_broadcast([P, tokens.stop - tokens.start, 2, 2]),
                in1=rows.rearrange("p o n h -> p n o h")[:, tokens],
                op=ALU.mult,
            )

        def add(s, engine, cols):
            if s not in dz_f:
                dz_f[s] = ring.tile([P, 1024], BF16, name="dz_f", tag="dz_f", align_bytes=64)
            flat = "p n o h -> p (n o h)"
            engine.tensor_tensor(
                out=dz_f[s][:, cols], in0=prod[s, 0][:].rearrange(flat)[:, cols], in1=prod[s, 1][:].rearrange(flat)[:, cols], op=ALU.add
            )

        def turn_back(s):
            t = s // 2
            if s % 2 == 0:
                back_ps[t] = [bank("back%d" % h, [P, 4, P]) for h in range(2)]
            words = dz_f[s][:].bitcast(F32)
            for h in range(2):
                for j in range(2):
                    nc.tensor.transpose(back_ps[t][h][:, 2 * (s % 2) + j, :], words[:, 256 * j + h : 256 * (j + 1) : 2], ident[:])

        def copy_on(engine, out, in_):
            if engine == "scalar":
                nc.scalar.copy(out=out, in_=in_)
            else:
                nc.vector.tensor_copy(out=out, in_=in_)

        def group_tokens(t, h, engine="scalar"):
            if h == 0:
                dz_t[t] = ring.tile([P, 4 * D], BF16, name="dz_t", tag="dz_t", align_bytes=64)
            src = back_ps[t][h][:].rearrange("p j r -> p (j r)").bitcast(BF16).rearrange("p (j c) -> p c j", j=4)
            copy_on(engine, dz_t[t][:, 2 * D * h : 2 * D * (h + 1)].rearrange("p (c j) -> p c j", j=4), src)

        def group_x(q):
            x_t[q] = ring.tile([P, 4 * D], BF16, name="x_t", tag="x_t", align_bytes=64)
            nc.scalar.copy(
                out=x_t[q][:].rearrange("p (c i j) -> p c j i", i=4, j=4),
                in_=x_raw[q][:].rearrange("p j (c i) -> p c j i", i=4),
            )

        def turn_w(w, b):
            words = w_raw[w][:].rearrange("r a f -> r (a f)").bitcast(F32)
            w_ps = bank("acc%d" % (2 * w + b), [P, 2, 2, P])
            for a in range(2):
                for h in range(2):
                    first = 256 * (2 * b + a)
                    nc.tensor.transpose(w_ps[:, a, h, :], words[:, first + h : first + 256 : 2], ident[:])
            if b == 0:
                w_t[w] = ring.tile([P, 4 * D], BF16, name="w_t", tag="w_t", align_bytes=64)
            dst = w_t[w][:].rearrange("p (a r o h) -> p a r o h", a=4, o=2, h=2)
            src = w_ps[:].rearrange("p a h r -> p (a h r)").bitcast(BF16).rearrange("p (a h r o) -> p a r o h", a=2, h=2, o=2)
            nc.scalar.copy(out=dst[:, 2 * b : 2 * b + 2], in_=src)

        def mx_pass(acc, still, still_fmt, cols, moving, moving_fmt, start, stop):
            nc.tensor.matmul_mx(
                out=acc[:],
                lhsT=still[0][:, cols].bitcast(still_fmt),
                lhsT_scale=still[1][:, cols],
                rhs=moving[0][:].bitcast(moving_fmt),
                rhs_scale=moving[1][:],
                start=start,
                stop=stop,
            )

        dx_ps, dw_ps = {}, {}

        def dx_mul(s, j, tag):
            dx_ps[s, j] = bank(tag, [P, D])
            for w in range(2):
                mx_pass(dx_ps[s, j], f_mx[s - 8 + 8 * w], E5M2, slice(P * j, P * (j + 1)), w_mx[w], E4M3, w == 0, w == 1)

        def dx_out(s, j, engine="scalar"):
            dx_sb = outs.tile([P, D], F32, name="out_sb", tag="out_sb")
            copy_on(engine, dx_sb[:], dx_ps[s, j][:])
            nc.sync.dma_start(out=dx_hbm[(s // 2) % SEQS][:, 2 * (s % 2) + j, :], in_=dx_sb[:])

        def dw_pass(w, m, q, tag):
            if q == 0:
                dw_ps[w, m] = bank(tag, [P, D])
            mx_pass(dw_ps[w, m], x_mx[q], E4M3, slice(P * m, P * (m + 1)), t_mx[SEQS * w + q], E5M2, q == 0, q == SEQS - 1)

        def dw_out(w, m, engine="scalar"):
            dw_sb = outs.tile([P, D], F32, name="out_sb", tag="out_sb")
            copy_on(
                engine,
                dw_sb[:].rearrange("p (c o) -> p c o", o=2),
                dw_ps[w, m][:].rearrange("p (o c) -> p c o", o=2),
            )
            nc.sync.dma_start(out=dw_hbm[w][P * m : P * (m + 1), :], in_=dw_sb[:])

        def quant_f(s):
            quantize(f_mx[s], E5M2, dz_f[s])

        def quant_t(t):
            quantize(t_mx[t], E5M2, dz_t[t])

        def quant_t_half(t, h):
            cols = slice(256 * h, 256 * (h + 1))
            nc.vector.quantize_mx(
                out=t_mx[t][0][:, cols].bitcast(E5M2), scales=t_mx[t][1][:, cols], in_=dz_t[t][:, 2 * D * h : 2 * D * (h + 1)]
            )

        group_x_slot = {0: 0, 4: 1, 6: 2, 8: 3}
        quant_x_slot = {2: 0, 5: 1, 7: 2, 9: 3}
        quant_w_slot = {3: 0, 10: 1}
        quant_t_slot = {4: 0, 6: 1, 8: 2, 9: 3, 12: 4, 13: 5}
        dwq_slot = {5: 0, 7: 1, 9: 2, 10: 3}
        pool_cols = slice(0, 1024 - VECTOR_SHARE)
        vector_cols = slice(1024 - VECTOR_SHARE, 1024)
        all_cols = slice(0, 1024)

        turn_g(0)
        turn_g(1)
        for s in range(STEPS):
            if s >= 1:
                add(s - 1, nc.gpsimd, pool_cols)
            product(s, 1)
            held = 2 * HELD_BACK if s == 14 else 0
            product(s, 0, slice(held, 256))
            if s >= 3 and s % 2 == 1 and s < 15:
                group_tokens((s - 3) // 2, 0)
                group_tokens((s - 3) // 2, 1)
            if s in group_x_slot:
                group_x(group_x_slot[s])
            if s == 0:
                turn_w(0, 0)
                turn_w(0, 1)
            if s in (1, 2):
                turn_w(1, s - 1)
            if s in dwq_slot:
                for m in range(4):
                    dw_pass(0, m, dwq_slot[s], "acc%d" % m)
            if s == 10:
                for m in range(4):
                    dw_out(0, m)
            if 11 <= s <= 14:
                for j in range(2):
                    dx_mul(s - 3, j, "acc%d" % (j + 2 * (s == 12)))
                    dx_out(s - 3, j)
            if s in (13, 14):
                for m in (2, 3):
                    dw_pass(1, m, s - 13, "acc%d" % m)
            if s == 14:
                dx_mul(12, 0, "acc0")
                dx_out(12, 0)
            if s == 15:
                dx_mul(12, 1, "acc1")
                dx_mul(13, 0, "fwd0")
                group_tokens(6, 0)
                dx_out(12, 1)
                dx_out(13, 0)
                group_tokens(6, 1)
                for m in (0, 1):
                    for q in (0, 1):
                        dw_pass(1, m, q, "acc%d" % m)
                dx_mul(13, 1, "fwd0")
                dx_out(13, 1)
            if s >= 1:
                add(s - 1, nc.vector, vector_cols)
            if s < 8:
                turn_g(s + 2)
            if 1 <= s <= 14:
                turn_back(s - 1)
            if 8 <= s < STEPS - 2:
                turn_g(s + 2)
            if s in quant_x_slot:
                quantize(x_mx[quant_x_slot[s]], E4M3, x_t[quant_x_slot[s]])
            if s in quant_w_slot:
                quantize(w_mx[quant_w_slot[s]], E4M3, w_t[quant_w_slot[s]])
            if s == 13:
                quant_t_half(5, 0)
                quant_f(12)
                quant_t_half(5, 1)
            elif s in quant_t_slot:
                quant_t(quant_t_slot[s])
            if 2 <= s <= 13:
                quant_f(s - 2)
            if s == 14:
                product(14, 0, slice(HELD_BACK, 2 * HELD_BACK))
                quant_f(13)
                product(14, 0, slice(0, HELD_BACK))

        quant_t_half(6, 0)
        quant_f(14)
        add(15, nc.vector, all_cols)
        dx_mul(14, 0, "fwd1")
        dx_out(14, 0)
        turn_back(14)
        turn_back(15)
        quant_f(15)
        quant_t_half(6, 1)
        group_tokens(7, 0)
        group_tokens(7, 1, "vector")
        dx_mul(14, 1, "fwd0")
        dx_out(14, 1)
        dx_mul(15, 0, "fwd1")
        dx_out(15, 0)
        dw_pass(1, 0, 2, None)
        quant_t_half(7, 0)
        quant_t_half(7, 1)
        dx_mul(15, 1, "back0")
        dx_out(15, 1, "vector")
        for m in range(4):
            if m > 0:
                dw_pass(1, m, 2, None)
            dw_pass(1, m, 3, None)
            dw_out(1, m, "scalar" if m % 2 == 0 else "vector")
